import numpy as np
import ml_dtypes


def mxq(x, axis, fmt="e4m3"):
    dtype, down = {"e4m3": (ml_dtypes.float8_e4m3fn, 7), "e5m2": (ml_dtypes.float8_e5m2, 14)}[fmt]
    v = np.moveaxis(np.asarray(x, np.float32).astype(ml_dtypes.bfloat16).astype(np.float64), axis, -1)
    blocks = v.reshape(v.shape[:-1] + (-1, 32))
    amax = np.abs(blocks).max(-1, keepdims=True)
    byte = np.maximum(np.where(amax > 0, np.frexp(amax)[1] - 1 + 127, 0) - down, 1)
    scale = np.exp2(byte - 127.0)
    codes = (blocks / scale).astype(np.float32).astype(dtype).astype(np.float64)
    return np.moveaxis((codes * scale).reshape(v.shape), -1, axis)


WIDE = False


def mx_kscale(k):
    if not WIDE:
        return np.ones(k)
    levels = np.array([10, -10, 5, -5, 0])
    if k % 512:
        return np.exp2(np.random.permutation(np.resize(levels, k // 32))).repeat(32)
    a = np.empty((k // 512, 16))
    for p in range(k // 512):
        a[p, :8] = np.random.permutation(np.resize(levels, 8))
        for g in range(8):
            far = levels[np.abs(levels - a[p, g]) >= 10]
            a[p, g + 8] = far[np.random.randint(len(far))]
    return np.exp2(a.ravel()).repeat(32)


BF16 = ml_dtypes.bfloat16


def bf(x):
    return np.asarray(x, np.float32).astype(BF16)


def f64(x):
    return np.asarray(x).astype(np.float64)


E2M1 = np.array([0.0, 0.5, 1.0, 1.5, 2.0, 3.0, 4.0, 6.0, -0.0, -0.5, -1.0, -1.5, -2.0, -3.0, -4.0, -6.0])


def pack_weight(w, fmt):
    k, n = w.shape
    w = f64(bf(w)).reshape(k // 32, 32, n)
    amax = np.abs(w).max(1)
    if fmt == "e4m3":
        byte = np.frexp(amax)[1] - 1 + 127 - 7
    else:
        mant, ex = np.frexp(amax / 6.0)
        byte = np.where(mant > 0.5, ex, ex - 1) + 127
    byte = np.clip(np.where(amax > 0, byte, 1), 1, 254)
    scaled = (w * np.exp2(127.0 - byte)[:, None, :]).reshape(k, n).astype(np.float32)
    by_word = np.ascontiguousarray(scaled.reshape(k // 512, 128, 4, n).transpose(0, 1, 3, 2))
    if fmt == "e4m3":
        words = by_word.astype(ml_dtypes.float8_e4m3fn).view(np.uint8)
    else:
        c = by_word.astype(ml_dtypes.float4_e2m1fn).view(np.uint8) & 0xF
        words = c[..., 0::2] | (c[..., 1::2] << 4)
    return np.ascontiguousarray(words), np.ascontiguousarray(byte.astype(np.uint8).reshape(k // 512, 16, n))


def unpack_weight(words, scales, fmt):
    g, p, n, _ = words.shape
    if fmt == "e4m3":
        vals = np.ascontiguousarray(words).view(ml_dtypes.float8_e4m3fn).astype(np.float64)
    else:
        nib = np.empty((g, p, n, 4), np.uint8)
        nib[..., 0::2] = words & 0xF
        nib[..., 1::2] = words >> 4
        vals = E2M1[nib]
    vals = vals * np.repeat(np.exp2(scales.astype(np.float64) - 127.0), 8, axis=1)[..., None]
    return vals.transpose(0, 1, 3, 2).reshape(g * 512, n)


B, F, H1, E, N, P, L, C, S = 8192, 2048, 1024, 512, 32, 8, 100, 16, 100
EPS = 1e-5


def layernorm(x, g, b):
    mu = x.mean(axis=-1, keepdims=True)
    var = x.var(axis=-1, keepdims=True)
    return (x - mu) / np.sqrt(var + EPS) * g + b


def setup_inputs():
    rn = np.random.standard_normal
    s = mx_kscale(H1)
    t = mx_kscale(E)
    h1 = bf(np.maximum(rn((B, H1)), 0.0) * s)
    W2_words, W2_scales = pack_weight(rn((H1, E)) / np.sqrt(H1) / s[:, None], "e4m3")
    return {"h1": h1,
            "W2_words": W2_words,
            "W2_scales": W2_scales,
            "b2": bf(rn(E) * 0.3),
            "ln_g": bf((1.0 + 0.2 * rn(E)) * t),
            "ln_b": bf(0.3 * rn(E) * t),
            "pc_W": bf(rn((N, E, P)) / np.sqrt(E) / t[None, :, None]),
            "pc_b": bf(0.3 * rn((N, P))),
            "pc_g": bf(1.0 + 0.2 * rn((N, P))),
            "pc_beta": bf(0.3 * rn((N, P)))}


def reference(h1, W2_words, W2_scales, b2, ln_g, ln_b, pc_W, pc_b, pc_g, pc_beta):
    z = np.maximum((mxq(f64(h1), 1, "e4m3") @ unpack_weight(W2_words, W2_scales, "e4m3")) + f64(b2), 0.0)
    h = layernorm(z, f64(ln_g), f64(ln_b))
    w = mxq(f64(pc_W), 1, "e4m3").transpose(1, 0, 2).reshape(E, N * P)
    prim = (mxq(h, 1, "e4m3") @ w).reshape(B, N, P) + f64(pc_b)[None]
    return layernorm(prim, f64(pc_g)[None], f64(pc_beta)[None])

@@ -1,0 +1,445 @@
+from contextlib import ExitStack
+
+import concourse.mybir as mybir
+from concourse.masks import make_identity
+
+F32 = mybir.dt.float32
+BF16 = mybir.dt.bfloat16
+I32 = mybir.dt.int32
+U32 = mybir.dt.uint32
+U8 = mybir.dt.uint8
+FP8X4 = mybir.dt.float8_e4m3fn_x4
+ACT = mybir.ActivationFunctionType
+ALU = mybir.AluOpType
+AXIS_X = mybir.AxisListType.X
+
+P = 128
+B, H1, E = 8192, 1024, 512
+CAPS, CAP_DIM = 32, 8
+OUT_COLS = CAPS * CAP_DIM
+EPS = 1e-5
+K_PASS = 4 * P
+PASSES_1 = H1 // K_PASS
+E_CHUNKS = E // P
+HALVES = OUT_COLS // P
+TILES = 2
+PAIR_ROWS = TILES * P
+N_PAIRS = B // PAIR_ROWS
+W_ROUND = 1
+
+FLOPS = 2 * B * (H1 * E + E * OUT_COLS)
+
+
+def tile_hotpatchcapsmodel_pa_t_kernel(
+    tc, h1, W2_words, W2_scales, b2, ln_g, ln_b, pc_W, pc_b, pc_g, pc_beta, out
+):
+    nc = tc.nc
+    with ExitStack() as stack:
+        const = stack.enter_context(tc.tile_pool(name="const", bufs=1))
+        setup = stack.enter_context(tc.tile_pool(name="setup", bufs=1))
+        loads = stack.enter_context(tc.tile_pool(name="loads", bufs=3))
+        work = stack.enter_context(tc.tile_pool(name="work", bufs=3))
+        small = stack.enter_context(tc.tile_pool(name="small", bufs=4))
+        psum = stack.enter_context(tc.psum_pool(name="psum", bufs=1))
+
+        x_tiles = {}
+
+        def load(i):
+            x_sb = loads.tile([P, TILES, H1], BF16, name="x_sb")
+            rows = h1[i * PAIR_ROWS : (i + 1) * PAIR_ROWS, :]
+            nc.sync.dma_start(out=x_sb[:], in_=rows.rearrange("(p j) k -> p j k", j=TILES))
+            x_tiles[i] = x_sb
+
+        load(0)
+
+        w2_scales_raw = setup.tile([P, PASSES_1, E], U8, name="w2_scales_raw", align_bytes=64)
+        nc.vector.memset(w2_scales_raw[:].bitcast(I32), 0)
+        for g in range(PASSES_1):
+            for quad in range(4):
+                nc.sync.dma_start(
+                    out=w2_scales_raw[32 * quad : 32 * quad + 4, g, :].bitcast(I32),
+                    in_=W2_scales[g, 4 * quad : 4 * quad + 4, :].bitcast(I32),
+                )
+        w2_codes_raw = setup.tile([P, PASSES_1, E], I32, name="w2_codes_raw", align_bytes=64)
+        for g in range(PASSES_1):
+            nc.sync.dma_start(
+                out=w2_codes_raw[:, g, :],
+                in_=W2_words[g].rearrange("p n t -> p (n t)").bitcast(I32),
+            )
+        w2_scales = const.tile([P, PASSES_1, E], U8, name="w2_scales", align_bytes=64)
+        w2_codes = const.tile([P, PASSES_1, E], U32, name="w2_codes", align_bytes=64)
+        for g in range(PASSES_1):
+            nc.vector.tensor_copy(
+                out=w2_scales[:, g, :].rearrange("p (t q) -> p q t", t=4),
+                in_=w2_scales_raw[:, g, :].rearrange("p (q t) -> p q t", t=4),
+            )
+            nc.vector.tensor_copy(
+                out=w2_codes[:, g, :].bitcast(I32).rearrange("p (t q) -> p t q", t=4),
+                in_=w2_codes_raw[:, g, :].rearrange("p (q t) -> p t q", t=4),
+            )
+
+        ident = const.tile([P, P], F32, name="ident")
+        make_identity(nc, ident[:])
+        eps_col = const.tile([P, 1], F32, name="eps_col")
+        nc.vector.memset(eps_col[:], EPS)
+
+
+        vec_rows = setup.tile([P, P], BF16, name="vec_rows")
+        nc.vector.memset(vec_rows[:], 0.0)
+        nc.scalar.dma_start(
+            out=vec_rows[0:HALVES, :], in_=pc_b.rearrange("n q -> (n q)").rearrange("(h q) -> h q", q=P)
+        )
+        b2_raw = setup.tile([P, E], BF16, name="b2_raw")
+        nc.scalar.dma_start(out=b2_raw[:], in_=b2.partition_broadcast(P))
+        b2_all = const.tile([P, E], BF16, name="b2_all")
+        nc.vector.tensor_copy(
+            out=b2_all[:].rearrange("p (t q) -> p t q", t=4), in_=b2_raw[:].rearrange("p (q t) -> p t q", t=4)
+        )
+        ln_g_raw = setup.tile([P, E_CHUNKS], BF16, name="ln_g_raw")
+        nc.scalar.dma_start(out=ln_g_raw[:], in_=ln_g.rearrange("(q t) -> q t", t=E_CHUNKS))
+        ln_b_raw = setup.tile([P, E_CHUNKS], BF16, name="ln_b_raw")
+        nc.scalar.dma_start(out=ln_b_raw[:], in_=ln_b.rearrange("(q t) -> q t", t=E_CHUNKS))
+        ln_g_cols = const.tile([P, E_CHUNKS], F32, name="ln_g_cols")
+        nc.vector.tensor_copy(out=ln_g_cols[:], in_=ln_g_raw[:])
+        ln_b_cols = const.tile([P, E_CHUNKS], F32, name="ln_b_cols")
+        nc.vector.tensor_copy(out=ln_b_cols[:], in_=ln_b_raw[:])
+        vec_rows_f = setup.tile([P, P], F32, name="vec_rows_f")
+        nc.vector.tensor_copy(out=vec_rows_f[:], in_=vec_rows[:])
+        vec_ps = psum.tile([P, P], F32, name="vec_ps", tag="xt", bufs=2)
+        nc.tensor.transpose(vec_ps[:], vec_rows_f[:], ident[:])
+        vec_cols = const.tile([P, HALVES], F32, name="vec_cols")
+        nc.vector.tensor_copy(out=vec_cols[:], in_=vec_ps[:, 0:HALVES])
+
+        def g1_col(c):
+            return ln_g_cols[:, c : c + 1]
+
+        def beta1_col(c):
+            return ln_b_cols[:, c : c + 1]
+
+        def pc_b_col(h):
+            return vec_cols[:, h : h + 1]
+
+        block_rows = setup.tile([P, P // CAP_DIM, CAP_DIM], F32, name="block_rows")
+        nc.vector.tensor_copy(
+            out=block_rows[:],
+            in_=ident[:, 0 : P // CAP_DIM].unsqueeze(2).to_broadcast([P, P // CAP_DIM, CAP_DIM]),
+        )
+        blocks_ps = psum.tile([P, P], F32, name="blocks_ps", tag="xt", bufs=2)
+        block_rows_2d = block_rows[:].rearrange("p n q -> p (n q)")
+        nc.tensor.matmul(out=blocks_ps[:], lhsT=block_rows_2d, rhs=block_rows_2d, start=True, stop=True)
+        centre = const.tile([P, P], F32, name="centre")
+        nc.vector.scalar_tensor_tensor(
+            out=centre[:], in0=blocks_ps[:], scalar=-1.0 / CAP_DIM, in1=ident[:], op0=ALU.mult, op1=ALU.add
+        )
+
+        w_raw = setup.tile([P, CAPS, E_CHUNKS, CAP_DIM], BF16, name="w_raw")
+        nc.scalar.dma_start(
+            out=w_raw[:].rearrange("p n t d -> p n (t d)"),
+            in_=pc_W.rearrange("n (q t) d -> q n (t d)", t=E_CHUNKS),
+        )
+        g2_all = const.tile([P, OUT_COLS], BF16, name="g2_all")
+        nc.scalar.dma_start(out=g2_all[:], in_=pc_g.rearrange("n q -> (n q)").partition_broadcast(P))
+        beta2_all = const.tile([P, OUT_COLS], BF16, name="beta2_all")
+        nc.scalar.dma_start(
+            out=beta2_all[:], in_=pc_beta.rearrange("n q -> (n q)").partition_broadcast(P)
+        )
+        w_codes = const.tile([P, OUT_COLS], U32, name="w_codes", align_bytes=64)
+        w_scales = const.tile([P, OUT_COLS], U8, name="w_scales", align_bytes=64)
+
+        def quantise_pc_w():
+            w_grouped = setup.tile([P, OUT_COLS, E_CHUNKS], BF16, name="w_grouped", align_bytes=64)
+            nc.vector.tensor_copy(
+                out=w_grouped[:].rearrange("p (n d) t -> p n d t", d=CAP_DIM),
+                in_=w_raw[:].rearrange("p n t d -> p n d t"),
+            )
+            nc.vector.quantize_mx(
+                out=w_codes[:].bitcast(FP8X4),
+                scales=w_scales[:],
+                in_=w_grouped[:].rearrange("p c t -> p (c t)"),
+            )
+
+        xt_tiles = {}
+        h1_grouped = {}
+        h1_q = {}
+        z_banks = {}
+        z_tiles = {}
+        z_sums = {}
+        neg_means = {}
+        dev_sqs = {}
+        rstds = {}
+        h_groupeds = {}
+        d_sq_sums = {}
+        y_tiles = {}
+        u_tiles = {}
+        uT_tiles = {}
+        h_planes = {}
+        h_q = {}
+        prim_banks = {}
+        xT_tiles = {}
+        d_banks = {}
+        d_squares = {}
+        rstd2_tiles = {}
+
+        def transpose_h1(i):
+            x_sb = x_tiles[i]
+            xt_tiles[i] = []
+            for j in range(TILES):
+                words = x_sb[:, j, :].bitcast(F32)
+                xt = psum.tile([P, PASSES_1, 2, P], F32, name="xt", tag="xt", bufs=2)
+                for g in range(PASSES_1):
+                    for u in range(2):
+                        nc.tensor.transpose(
+                            xt[:, g, u, :], words[:, 256 * g + u : 256 * (g + 1) : 2], ident[:]
+                        )
+                xt_tiles[i].append(xt)
+
+        def copy_h1(i):
+            grouped = work.tile([P, TILES, PASSES_1, P, 4], BF16, name="h1_grouped", align_bytes=64)
+            for j in range(TILES):
+                nc.scalar.copy(
+                    out=grouped[:, j].bitcast(F32), in_=xt_tiles[i][j][:].rearrange("p g u b -> p g b u")
+                )
+            h1_grouped[i] = grouped
+
+        def quantise_h1(i):
+            codes = work.tile([P, TILES * PASSES_1 * P], U32, name="h1_codes", align_bytes=64)
+            scales = work.tile([P, TILES * PASSES_1 * P], U8, name="h1_scales", align_bytes=64)
+            nc.vector.quantize_mx(
+                out=codes[:].bitcast(FP8X4),
+                scales=scales[:],
+                in_=h1_grouped[i][:].rearrange("p j g b t -> p (j g b t)"),
+            )
+            h1_q[i] = (codes, scales)
+
+        def product_1(i):
+            codes, scales = h1_q[i]
+            z_banks[i] = []
+            for j in range(TILES):
+                z_ps = psum.tile([P, E], F32, name="z_ps", tag="z_ps", bufs=2)
+                for g in range(PASSES_1):
+                    cols = slice((j * PASSES_1 + g) * P, (j * PASSES_1 + g + 1) * P)
+                    nc.tensor.matmul_mx(
+                        out=z_ps[:],
+                        lhsT=codes[:, cols].bitcast(FP8X4),
+                        lhsT_scale=scales[:, cols],
+                        rhs=w2_codes[:, g, :].bitcast(FP8X4),
+                        rhs_scale=w2_scales[:, g, :],
+                        start=(g == 0),
+                        stop=(g == PASSES_1 - 1),
+                    )
+                z_banks[i].append(z_ps)
+
+        def add_bias(i):
+            z = work.tile([P, TILES, E], F32, name="z")
+            for j in range(TILES):
+                nc.vector.tensor_tensor(out=z[:, j, :], in0=z_banks[i][j][:], in1=b2_all[:], op=ALU.add)
+            z_tiles[i] = z
+
+        def relu(i):
+            z = z_tiles[i]
+            z_sum = small.tile([P, TILES], F32, name="z_sum")
+            for j in range(TILES):
+                nc.scalar.activation(
+                    out=z[:, j, :], in_=z[:, j, :], func=ACT.Relu, accum_out=z_sum[:, j : j + 1]
+                )
+            z_sums[i] = z_sum
+
+        def mean(i):
+            neg_mean = small.tile([P, TILES], F32, name="neg_mean")
+            nc.scalar.mul(out=neg_mean[:], in_=z_sums[i][:], mul=-1.0 / E)
+            neg_means[i] = neg_mean
+
+        def deviations(i):
+            dev_sq = small.tile([P, TILES], F32, name="dev_sq")
+            for j in range(TILES):
+                unread = work.tile([P, E], F32, name="unread")
+                nc.scalar.activation(
+                    out=unread[:],
+                    in_=z_tiles[i][:, j, :],
+                    func=ACT.Square,
+                    bias=neg_means[i][:, j : j + 1],
+                    accum_out=dev_sq[:, j : j + 1],
+                )
+            dev_sqs[i] = dev_sq
+
+        def rstd_1(i):
+            rstd = small.tile([P, TILES], F32, name="rstd")
+            nc.scalar.activation(
+                out=rstd[:], in_=dev_sqs[i][:], func=ACT.Abs_reciprocal_sqrt, bias=eps_col[:], scale=1.0 / E
+            )
+            rstds[i] = rstd
+
+        def normalise(i):
+            z = z_tiles[i]
+            neg_mean, rstd = neg_means[i], rstds[i]
+            u = work.tile([P, TILES, E], F32, name="u")
+            for j in range(TILES):
+                nc.vector.tensor_scalar(
+                    out=u[:, j, :],
+                    in0=z[:, j, :],
+                    scalar1=neg_mean[:, j : j + 1],
+                    scalar2=rstd[:, j : j + 1],
+                    op0=ALU.add,
+                    op1=ALU.mult,
+                )
+            u_tiles[i] = u
+
+        def transpose_u(i):
+            u = u_tiles[i]
+            uT_tiles[i] = []
+            for half in range(2):
+                uT = psum.tile([P, 2, TILES, P], F32, name="uT", tag="uT", bufs=2)
+                for cc in range(2):
+                    c = 2 * half + cc
+                    for j in range(TILES):
+                        nc.tensor.transpose(uT[:, cc, j, :], u[:, j, c * P : (c + 1) * P], ident[:])
+                uT_tiles[i].append(uT)
+
+        def gain_shift(i, half):
+            if half == 0:
+                planes = work.tile([P, E_CHUNKS, PAIR_ROWS], BF16, name="h_planes")
+                h_planes[i] = planes
+            for cc in range(2):
+                c = 2 * half + cc
+                nc.scalar.activation(
+                    out=h_planes[i][:, c, :],
+                    in_=uT_tiles[i][half][:, cc].rearrange("p j b -> p (j b)"),
+                    func=ACT.Identity,
+                    scale=g1_col(c),
+                    bias=beta1_col(c),
+                )
+
+        def regroup_h(i):
+            grouped = work.tile([P, PAIR_ROWS, E_CHUNKS], BF16, name="h_grouped", align_bytes=64)
+            nc.vector.tensor_copy(
+                out=grouped[:].rearrange("p (c i) t -> p c t i", i=4),
+                in_=h_planes[i][:].rearrange("p t (c i) -> p c t i", i=4),
+            )
+            h_groupeds[i] = grouped
+
+        def quantise_h(i):
+            codes = work.tile([P, PAIR_ROWS], U32, name="h_codes", align_bytes=64)
+            scales = work.tile([P, PAIR_ROWS], U8, name="h_scales", align_bytes=64)
+            nc.vector.quantize_mx(
+                out=codes[:].bitcast(FP8X4),
+                scales=scales[:],
+                in_=h_groupeds[i][:].rearrange("p b t -> p (b t)"),
+            )
+            h_q[i] = (codes, scales)
+
+        def product_2(i):
+            codes, scales = h_q[i]
+            prim_ps = psum.tile([P, HALVES, PAIR_ROWS], F32, name="prim_ps", tag="prim_ps", bufs=1)
+            for h in range(HALVES):
+                nc.tensor.matmul_mx(
+                    out=prim_ps[:, h, :],
+                    lhsT=w_codes[:, h * P : (h + 1) * P].bitcast(FP8X4),
+                    lhsT_scale=w_scales[:, h * P : (h + 1) * P],
+                    rhs=codes[:].bitcast(FP8X4),
+                    rhs_scale=scales[:],
+                    start=True,
+                    stop=True,
+                )
+            prim_banks[i] = prim_ps
+
+        def capsule_bias(i):
+            xT = work.tile([P, HALVES, PAIR_ROWS], F32, name="xT")
+            nc.scalar.activation(out=xT[:, 0, :], in_=prim_banks[i][:, 0, :], func=ACT.Identity, bias=pc_b_col(0))
+            nc.vector.tensor_scalar_add(out=xT[:, 1, :], in0=prim_banks[i][:, 1, :], scalar1=pc_b_col(1))
+            xT_tiles[i] = xT
+
+        def centre_capsules(i):
+            xT = xT_tiles[i]
+            d_ps = psum.tile([P, TILES, OUT_COLS], F32, name="d_ps", tag="d_ps", bufs=1)
+            for j in range(TILES):
+                for h in range(HALVES):
+                    nc.tensor.matmul(
+                        out=d_ps[:, j, h * P : (h + 1) * P],
+                        lhsT=xT[:, h, j * P : (j + 1) * P],
+                        rhs=centre[:],
+                        start=True,
+                        stop=True,
+                    )
+            d_banks[i] = d_ps
+
+        def square_capsules(i):
+            d_sq = work.tile([P, TILES * CAPS, CAP_DIM], F32, name="d_sq")
+            nc.scalar.activation(
+                out=d_sq[:].rearrange("p c q -> p (c q)"),
+                in_=d_banks[i][:].rearrange("p j c -> p (j c)"),
+                func=ACT.Square,
+            )
+            d_squares[i] = d_sq
+
+        def reduce_2(i):
+            d_sq_sum = small.tile([P, TILES * CAPS], F32, name="d_sq_sum")
+            nc.vector.reduce_sum(out=d_sq_sum[:], in_=d_squares[i][:], axis=AXIS_X)
+            d_sq_sums[i] = d_sq_sum
+
+        def rstd_2(i):
+            rstd2 = small.tile([P, TILES * CAPS], F32, name="rstd2")
+            nc.scalar.activation(
+                out=rstd2[:],
+                in_=d_sq_sums[i][:],
+                func=ACT.Abs_reciprocal_sqrt,
+                bias=eps_col[:],
+                scale=1.0 / CAP_DIM,
+            )
+            rstd2_tiles[i] = rstd2
+
+        def scale_2(i):
+            y = work.tile([P, TILES, OUT_COLS], F32, name="y")
+            nc.vector.tensor_tensor(
+                out=y[:].rearrange("p j (n q) -> p (j n) q", q=CAP_DIM),
+                in0=d_banks[i][:].rearrange("p j (n q) -> p (j n) q", q=CAP_DIM),
+                in1=rstd2_tiles[i][:].unsqueeze(2).to_broadcast([P, TILES * CAPS, CAP_DIM]),
+                op=ALU.mult,
+            )
+            y_tiles[i] = y
+
+        def gain_2(i):
+            y = y_tiles[i]
+            nc.vector.tensor_tensor(
+                out=y[:], in0=y[:], in1=g2_all[:].unsqueeze(1).to_broadcast([P, TILES, OUT_COLS]), op=ALU.mult
+            )
+
+        def shift_2(i):
+            y = y_tiles[i]
+            nc.vector.tensor_tensor(
+                out=y[:], in0=y[:], in1=beta2_all[:].unsqueeze(1).to_broadcast([P, TILES, OUT_COLS]), op=ALU.add
+            )
+            rows = out[i * PAIR_ROWS : (i + 1) * PAIR_ROWS, :, :]
+            nc.sync.dma_start(out=rows.rearrange("(p j) n q -> p j (n q)", j=TILES), in_=y[:])
+
+        def run(step, i, *args):
+            if 0 <= i < N_PAIRS:
+                step(i, *args)
+
+        for r in range(-1, N_PAIRS + 6):
+            run(load, r + 2)
+            run(normalise, r - 2)
+            run(copy_h1, r)
+            run(centre_capsules, r - 5)
+            run(gain_2, r - 6)
+            run(relu, r - 1)
+            run(transpose_h1, r + 1)
+            run(quantise_h1, r)
+            if r == W_ROUND:
+                quantise_pc_w()
+            run(square_capsules, r - 5)
+            run(mean, r - 1)
+            run(shift_2, r - 6)
+            run(product_1, r)
+            run(regroup_h, r - 4)
+            run(gain_shift, r - 3, 0)
+            run(gain_shift, r - 3, 1)
+            run(reduce_2, r - 5)
+            run(quantise_h, r - 4)
+            run(product_2, r - 4)
+            run(rstd_2, r - 5)
+            run(transpose_u, r - 2)
+            run(deviations, r - 1)
+            run(scale_2, r - 5)
+            run(add_bias, r)
+            run(capsule_bias, r - 4)
+            run(rstd_1, r - 1)

@@ -344,8 +344,8 @@ def tile_hotpatchcapsmodel_pa_t_kernel(
 
         def capsule_bias(i):
             xT = work.tile([P, HALVES, PAIR_ROWS], F32, name="xT")
-            nc.scalar.activation(out=xT[:, 0, :], in_=prim_banks[i][:, 0, :], func=ACT.Identity, bias=pc_b_col(0))
-            nc.vector.tensor_scalar_add(out=xT[:, 1, :], in0=prim_banks[i][:, 1, :], scalar1=pc_b_col(1))
+            for h in range(HALVES):
+                nc.vector.tensor_scalar_add(out=xT[:, h, :], in0=prim_banks[i][:, h, :], scalar1=pc_b_col(h))
             xT_tiles[i] = xT
 
         def centre_capsules(i):
@@ -399,13 +399,13 @@ def tile_hotpatchcapsmodel_pa_t_kernel(
 
         def gain_2(i):
             y = y_tiles[i]
-            nc.vector.tensor_tensor(
+            nc.gpsimd.tensor_tensor(
                 out=y[:], in0=y[:], in1=g2_all[:].unsqueeze(1).to_broadcast([P, TILES, OUT_COLS]), op=ALU.mult
             )
 
         def shift_2(i):
             y = y_tiles[i]
-            nc.vector.tensor_tensor(
+            nc.gpsimd.tensor_tensor(
                 out=y[:], in0=y[:], in1=beta2_all[:].unsqueeze(1).to_broadcast([P, TILES, OUT_COLS]), op=ALU.add
             )
             rows = out[i * PAIR_ROWS : (i + 1) * PAIR_ROWS, :, :]

@@ -18,6 +18,7 @@ B, H1, E = 8192, 1024, 512
 CAPS, CAP_DIM = 32, 8
 OUT_COLS = CAPS * CAP_DIM
 EPS = 1e-5
+F32_MAX = 3.4028234663852886e38
 K_PASS = 4 * P
 PASSES_1 = H1 // K_PASS
 E_CHUNKS = E // P
@@ -163,9 +164,7 @@ def tile_hotpatchcapsmodel_pa_t_kernel(
         h1_q = {}
         z_banks = {}
         z_tiles = {}
-        z_sums = {}
-        neg_means = {}
-        dev_sqs = {}
+        stats_tiles = {}
         rstds = {}
         h_groupeds = {}
         d_sq_sums = {}
@@ -237,49 +236,37 @@ def tile_hotpatchcapsmodel_pa_t_kernel(
 
         def relu(i):
             z = z_tiles[i]
-            z_sum = small.tile([P, TILES], F32, name="z_sum")
-            for j in range(TILES):
-                nc.scalar.activation(
-                    out=z[:, j, :], in_=z[:, j, :], func=ACT.Relu, accum_out=z_sum[:, j : j + 1]
-                )
-            z_sums[i] = z_sum
+            nc.gpsimd.tensor_scalar(
+                out=z[:], in0=z[:], scalar1=F32_MAX, scalar2=0.0, op0=ALU.min, op1=ALU.max
+            )
 
-        def mean(i):
-            neg_mean = small.tile([P, TILES], F32, name="neg_mean")
-            nc.scalar.mul(out=neg_mean[:], in_=z_sums[i][:], mul=-1.0 / E)
-            neg_means[i] = neg_mean
-
-        def deviations(i):
-            dev_sq = small.tile([P, TILES], F32, name="dev_sq")
+        def row_stats(i):
+            halves = small.tile([P, TILES, 6], F32, name="stat_halves")
+            stats = small.tile([P, TILES, 2], F32, name="stats")
             for j in range(TILES):
-                unread = work.tile([P, E], F32, name="unread")
-                nc.scalar.activation(
-                    out=unread[:],
-                    in_=z_tiles[i][:, j, :],
-                    func=ACT.Square,
-                    bias=neg_means[i][:, j : j + 1],
-                    accum_out=dev_sq[:, j : j + 1],
-                )
-            dev_sqs[i] = dev_sq
+                nc.vector.bn_stats(out=halves[:, j, :], in_=z_tiles[i][:, j, :])
+            for j in range(TILES):
+                nc.vector.bn_aggr(out=stats[:, j, :], in_=halves[:, j, :])
+            stats_tiles[i] = stats
 
         def rstd_1(i):
             rstd = small.tile([P, TILES], F32, name="rstd")
             nc.scalar.activation(
-                out=rstd[:], in_=dev_sqs[i][:], func=ACT.Abs_reciprocal_sqrt, bias=eps_col[:], scale=1.0 / E
+                out=rstd[:], in_=stats_tiles[i][:, :, 1], func=ACT.Abs_reciprocal_sqrt, bias=eps_col[:]
             )
             rstds[i] = rstd
 
         def normalise(i):
             z = z_tiles[i]
-            neg_mean, rstd = neg_means[i], rstds[i]
+            stats, rstd = stats_tiles[i], rstds[i]
             u = work.tile([P, TILES, E], F32, name="u")
             for j in range(TILES):
                 nc.vector.tensor_scalar(
                     out=u[:, j, :],
                     in0=z[:, j, :],
-                    scalar1=neg_mean[:, j : j + 1],
+                    scalar1=stats[:, j, 0:1],
                     scalar2=rstd[:, j : j + 1],
-                    op0=ALU.add,
+                    op0=ALU.subtract,
                     op1=ALU.mult,
                 )
             u_tiles[i] = u
@@ -311,7 +298,7 @@ def tile_hotpatchcapsmodel_pa_t_kernel(
 
         def regroup_h(i):
             grouped = work.tile([P, PAIR_ROWS, E_CHUNKS], BF16, name="h_grouped", align_bytes=64)
-            nc.vector.tensor_copy(
+            nc.scalar.copy(
                 out=grouped[:].rearrange("p (c i) t -> p c t i", i=4),
                 in_=h_planes[i][:].rearrange("p t (c i) -> p c t i", i=4),
             )
@@ -345,7 +332,7 @@ def tile_hotpatchcapsmodel_pa_t_kernel(
         def capsule_bias(i):
             xT = work.tile([P, HALVES, PAIR_ROWS], F32, name="xT")
             for h in range(HALVES):
-                nc.vector.tensor_scalar_add(out=xT[:, h, :], in0=prim_banks[i][:, h, :], scalar1=pc_b_col(h))
+                nc.scalar.activation(out=xT[:, h, :], in_=prim_banks[i][:, h, :], func=ACT.Identity, bias=pc_b_col(h))
             xT_tiles[i] = xT
 
         def centre_capsules(i):
@@ -427,7 +414,6 @@ def tile_hotpatchcapsmodel_pa_t_kernel(
             if r == W_ROUND:
                 quantise_pc_w()
             run(square_capsules, r - 5)
-            run(mean, r - 1)
             run(shift_2, r - 6)
             run(product_1, r)
             run(regroup_h, r - 4)
@@ -438,7 +424,7 @@ def tile_hotpatchcapsmodel_pa_t_kernel(
             run(product_2, r - 4)
             run(rstd_2, r - 5)
             run(transpose_u, r - 2)
-            run(deviations, r - 1)
+            run(row_stats, r - 1)
             run(scale_2, r - 5)
             run(add_bias, r)
             run(capsule_bias, r - 4)

@@ -26,6 +26,7 @@ HALVES = OUT_COLS // P
 TILES = 2
 PAIR_ROWS = TILES * P
 N_PAIRS = B // PAIR_ROWS
+SHARED_BANKS = 5
 W_ROUND = 1
 
 FLOPS = 2 * B * (H1 * E + E * OUT_COLS)
@@ -106,7 +107,7 @@ def tile_hotpatchcapsmodel_pa_t_kernel(
         nc.vector.tensor_copy(out=ln_b_cols[:], in_=ln_b_raw[:])
         vec_rows_f = setup.tile([P, P], F32, name="vec_rows_f")
         nc.vector.tensor_copy(out=vec_rows_f[:], in_=vec_rows[:])
-        vec_ps = psum.tile([P, P], F32, name="vec_ps", tag="xt", bufs=2)
+        vec_ps = psum.tile([P, P], F32, name="vec_ps", tag="bank", bufs=SHARED_BANKS)
         nc.tensor.transpose(vec_ps[:], vec_rows_f[:], ident[:])
         vec_cols = const.tile([P, HALVES], F32, name="vec_cols")
         nc.vector.tensor_copy(out=vec_cols[:], in_=vec_ps[:, 0:HALVES])
@@ -125,7 +126,7 @@ def tile_hotpatchcapsmodel_pa_t_kernel(
             out=block_rows[:],
             in_=ident[:, 0 : P // CAP_DIM].unsqueeze(2).to_broadcast([P, P // CAP_DIM, CAP_DIM]),
         )
-        blocks_ps = psum.tile([P, P], F32, name="blocks_ps", tag="xt", bufs=2)
+        blocks_ps = psum.tile([P, P], F32, name="blocks_ps", tag="bank", bufs=SHARED_BANKS)
         block_rows_2d = block_rows[:].rearrange("p n q -> p (n q)")
         nc.tensor.matmul(out=blocks_ps[:], lhsT=block_rows_2d, rhs=block_rows_2d, start=True, stop=True)
         centre = const.tile([P, P], F32, name="centre")
@@ -184,7 +185,7 @@ def tile_hotpatchcapsmodel_pa_t_kernel(
             xt_tiles[i] = []
             for j in range(TILES):
                 words = x_sb[:, j, :].bitcast(F32)
-                xt = psum.tile([P, PASSES_1, 2, P], F32, name="xt", tag="xt", bufs=2)
+                xt = psum.tile([P, PASSES_1, 2, P], F32, name="xt", tag="bank", bufs=SHARED_BANKS)
                 for g in range(PASSES_1):
                     for u in range(2):
                         nc.tensor.transpose(
@@ -214,7 +215,7 @@ def tile_hotpatchcapsmodel_pa_t_kernel(
             codes, scales = h1_q[i]
             z_banks[i] = []
             for j in range(TILES):
-                z_ps = psum.tile([P, E], F32, name="z_ps", tag="z_ps", bufs=2)
+                z_ps = psum.tile([P, E], F32, name="z_ps", tag="bank", bufs=SHARED_BANKS)
                 for g in range(PASSES_1):
                     cols = slice((j * PASSES_1 + g) * P, (j * PASSES_1 + g + 1) * P)
                     nc.tensor.matmul_mx(
@@ -275,7 +276,7 @@ def tile_hotpatchcapsmodel_pa_t_kernel(
             u = u_tiles[i]
             uT_tiles[i] = []
             for half in range(2):
-                uT = psum.tile([P, 2, TILES, P], F32, name="uT", tag="uT", bufs=2)
+                uT = psum.tile([P, 2, TILES, P], F32, name="uT", tag="bank", bufs=SHARED_BANKS)
                 for cc in range(2):
                     c = 2 * half + cc
                     for j in range(TILES):
@@ -337,7 +338,7 @@ def tile_hotpatchcapsmodel_pa_t_kernel(
 
         def centre_capsules(i):
             xT = xT_tiles[i]
-            d_ps = psum.tile([P, TILES, OUT_COLS], F32, name="d_ps", tag="d_ps", bufs=1)
+            d_ps = psum.tile([P, TILES, OUT_COLS], F32, name="d_ps", tag="d_ps", bufs=2)
             for j in range(TILES):
                 for h in range(HALVES):
                     nc.tensor.matmul(

@@ -27,7 +27,7 @@ TILES = 2
 PAIR_ROWS = TILES * P
 N_PAIRS = B // PAIR_ROWS
 SHARED_BANKS = 5
-W_ROUND = 1
+W_ROUND = 2
 
 FLOPS = 2 * B * (H1 * E + E * OUT_COLS)
 
@@ -44,30 +44,47 @@ def tile_hotpatchcapsmodel_pa_t_kernel(
         small = stack.enter_context(tc.tile_pool(name="small", bufs=4))
         psum = stack.enter_context(tc.psum_pool(name="psum", bufs=1))
 
+        def parts(i):
+            if i in (0, N_PAIRS - 1):
+                return [slice(j, j + 1) for j in range(TILES)]
+            return [slice(0, TILES)]
+
+        def columns(part, width):
+            return slice(part.start * width, part.stop * width)
+
         x_tiles = {}
 
         def load(i):
             x_sb = loads.tile([P, TILES, H1], BF16, name="x_sb")
-            rows = h1[i * PAIR_ROWS : (i + 1) * PAIR_ROWS, :]
-            nc.sync.dma_start(out=x_sb[:], in_=rows.rearrange("(p j) k -> p j k", j=TILES))
+            rows = h1[i * PAIR_ROWS : (i + 1) * PAIR_ROWS, :].rearrange("(p j) k -> p j k", j=TILES)
+            for part in parts(i):
+                nc.sync.dma_start(out=x_sb[:, part], in_=rows[:, part])
             x_tiles[i] = x_sb
+
+        eps_col = const.tile([P, 1], F32, name="eps_col")
+        nc.vector.memset(eps_col[:], EPS)
+        first_act = const.tile([P, 1], F32, name="first_act")
+        nc.scalar.activation(out=first_act[:], in_=eps_col[:], func=ACT.Abs_reciprocal_sqrt)
+        ident = const.tile([P, P], F32, name="ident")
+        make_identity(nc, ident[:])
 
         load(0)
 
         w2_scales_raw = setup.tile([P, PASSES_1, E], U8, name="w2_scales_raw", align_bytes=64)
         nc.vector.memset(w2_scales_raw[:].bitcast(I32), 0)
-        for g in range(PASSES_1):
-            for quad in range(4):
-                nc.sync.dma_start(
-                    out=w2_scales_raw[32 * quad : 32 * quad + 4, g, :].bitcast(I32),
-                    in_=W2_scales[g, 4 * quad : 4 * quad + 4, :].bitcast(I32),
-                )
+        for quad in range(4):
+            nc.sync.dma_start(
+                out=w2_scales_raw[32 * quad : 32 * quad + 4, :, :].bitcast(I32),
+                in_=W2_scales[:, 4 * quad : 4 * quad + 4, :].rearrange("g q n -> q g n").bitcast(I32),
+            )
         w2_codes_raw = setup.tile([P, PASSES_1, E], I32, name="w2_codes_raw", align_bytes=64)
         for g in range(PASSES_1):
             nc.sync.dma_start(
                 out=w2_codes_raw[:, g, :],
                 in_=W2_words[g].rearrange("p n t -> p (n t)").bitcast(I32),
             )
+        b2_raw = setup.tile([P, E], BF16, name="b2_raw")
+        nc.sync.dma_start(out=b2_raw[:], in_=b2.partition_broadcast(P))
         w2_scales = const.tile([P, PASSES_1, E], U8, name="w2_scales", align_bytes=64)
         w2_codes = const.tile([P, PASSES_1, E], U32, name="w2_codes", align_bytes=64)
         for g in range(PASSES_1):
@@ -79,38 +96,23 @@ def tile_hotpatchcapsmodel_pa_t_kernel(
                 out=w2_codes[:, g, :].bitcast(I32).rearrange("p (t q) -> p t q", t=4),
                 in_=w2_codes_raw[:, g, :].rearrange("p (q t) -> p t q", t=4),
             )
-
-        ident = const.tile([P, P], F32, name="ident")
-        make_identity(nc, ident[:])
-        eps_col = const.tile([P, 1], F32, name="eps_col")
-        nc.vector.memset(eps_col[:], EPS)
-
-
-        vec_rows = setup.tile([P, P], BF16, name="vec_rows")
-        nc.vector.memset(vec_rows[:], 0.0)
-        nc.scalar.dma_start(
-            out=vec_rows[0:HALVES, :], in_=pc_b.rearrange("n q -> (n q)").rearrange("(h q) -> h q", q=P)
-        )
-        b2_raw = setup.tile([P, E], BF16, name="b2_raw")
-        nc.scalar.dma_start(out=b2_raw[:], in_=b2.partition_broadcast(P))
         b2_all = const.tile([P, E], BF16, name="b2_all")
         nc.vector.tensor_copy(
             out=b2_all[:].rearrange("p (t q) -> p t q", t=4), in_=b2_raw[:].rearrange("p (q t) -> p t q", t=4)
         )
-        ln_g_raw = setup.tile([P, E_CHUNKS], BF16, name="ln_g_raw")
-        nc.scalar.dma_start(out=ln_g_raw[:], in_=ln_g.rearrange("(q t) -> q t", t=E_CHUNKS))
-        ln_b_raw = setup.tile([P, E_CHUNKS], BF16, name="ln_b_raw")
-        nc.scalar.dma_start(out=ln_b_raw[:], in_=ln_b.rearrange("(q t) -> q t", t=E_CHUNKS))
+
         ln_g_cols = const.tile([P, E_CHUNKS], F32, name="ln_g_cols")
-        nc.vector.tensor_copy(out=ln_g_cols[:], in_=ln_g_raw[:])
         ln_b_cols = const.tile([P, E_CHUNKS], F32, name="ln_b_cols")
-        nc.vector.tensor_copy(out=ln_b_cols[:], in_=ln_b_raw[:])
-        vec_rows_f = setup.tile([P, P], F32, name="vec_rows_f")
-        nc.vector.tensor_copy(out=vec_rows_f[:], in_=vec_rows[:])
-        vec_ps = psum.tile([P, P], F32, name="vec_ps", tag="bank", bufs=SHARED_BANKS)
-        nc.tensor.transpose(vec_ps[:], vec_rows_f[:], ident[:])
         vec_cols = const.tile([P, HALVES], F32, name="vec_cols")
-        nc.vector.tensor_copy(out=vec_cols[:], in_=vec_ps[:, 0:HALVES])
+        centre = const.tile([P, P], F32, name="centre")
+        w_codes = const.tile([P, OUT_COLS], U32, name="w_codes", align_bytes=64)
+        w_scales = const.tile([P, OUT_COLS], U8, name="w_scales", align_bytes=64)
+        g2_all = const.tile([P, OUT_COLS], BF16, name="g2_all")
+        beta2_all = const.tile([P, OUT_COLS], BF16, name="beta2_all")
+        w_raw = setup.tile([P, CAPS, E_CHUNKS, CAP_DIM], BF16, name="w_raw")
+        ln_g_raw = setup.tile([P, E_CHUNKS], BF16, name="ln_g_raw")
+        ln_b_raw = setup.tile([P, E_CHUNKS], BF16, name="ln_b_raw")
+        vec_rows = setup.tile([P, P], BF16, name="vec_rows")
 
         def g1_col(c):
             return ln_g_cols[:, c : c + 1]
@@ -121,43 +123,48 @@ def tile_hotpatchcapsmodel_pa_t_kernel(
         def pc_b_col(h):
             return vec_cols[:, h : h + 1]
 
-        block_rows = setup.tile([P, P // CAP_DIM, CAP_DIM], F32, name="block_rows")
-        nc.vector.tensor_copy(
-            out=block_rows[:],
-            in_=ident[:, 0 : P // CAP_DIM].unsqueeze(2).to_broadcast([P, P // CAP_DIM, CAP_DIM]),
-        )
-        blocks_ps = psum.tile([P, P], F32, name="blocks_ps", tag="bank", bufs=SHARED_BANKS)
-        block_rows_2d = block_rows[:].rearrange("p n q -> p (n q)")
-        nc.tensor.matmul(out=blocks_ps[:], lhsT=block_rows_2d, rhs=block_rows_2d, start=True, stop=True)
-        centre = const.tile([P, P], F32, name="centre")
-        nc.vector.scalar_tensor_tensor(
-            out=centre[:], in0=blocks_ps[:], scalar=-1.0 / CAP_DIM, in1=ident[:], op0=ALU.mult, op1=ALU.add
-        )
+        def load_late_constants():
+            nc.sync.dma_start(
+                out=w_raw[:].rearrange("p n t d -> p n (t d)"),
+                in_=pc_W.rearrange("n (q t) d -> q n (t d)", t=E_CHUNKS),
+            )
+            nc.sync.dma_start(out=ln_g_raw[:], in_=ln_g.rearrange("(q t) -> q t", t=E_CHUNKS))
+            nc.sync.dma_start(out=ln_b_raw[:], in_=ln_b.rearrange("(q t) -> q t", t=E_CHUNKS))
+            nc.vector.memset(vec_rows[:], 0.0)
+            nc.sync.dma_start(
+                out=vec_rows[0:HALVES, :], in_=pc_b.rearrange("n q -> (n q)").rearrange("(h q) -> h q", q=P)
+            )
+            nc.sync.dma_start(out=g2_all[:], in_=pc_g.rearrange("n q -> (n q)").partition_broadcast(P))
+            nc.sync.dma_start(out=beta2_all[:], in_=pc_beta.rearrange("n q -> (n q)").partition_broadcast(P))
 
-        w_raw = setup.tile([P, CAPS, E_CHUNKS, CAP_DIM], BF16, name="w_raw")
-        nc.scalar.dma_start(
-            out=w_raw[:].rearrange("p n t d -> p n (t d)"),
-            in_=pc_W.rearrange("n (q t) d -> q n (t d)", t=E_CHUNKS),
-        )
-        g2_all = const.tile([P, OUT_COLS], BF16, name="g2_all")
-        nc.scalar.dma_start(out=g2_all[:], in_=pc_g.rearrange("n q -> (n q)").partition_broadcast(P))
-        beta2_all = const.tile([P, OUT_COLS], BF16, name="beta2_all")
-        nc.scalar.dma_start(
-            out=beta2_all[:], in_=pc_beta.rearrange("n q -> (n q)").partition_broadcast(P)
-        )
-        w_codes = const.tile([P, OUT_COLS], U32, name="w_codes", align_bytes=64)
-        w_scales = const.tile([P, OUT_COLS], U8, name="w_scales", align_bytes=64)
-
-        def quantise_pc_w():
+        def prepare_late_constants():
             w_grouped = setup.tile([P, OUT_COLS, E_CHUNKS], BF16, name="w_grouped", align_bytes=64)
             nc.vector.tensor_copy(
                 out=w_grouped[:].rearrange("p (n d) t -> p n d t", d=CAP_DIM),
                 in_=w_raw[:].rearrange("p n t d -> p n d t"),
             )
+            nc.vector.tensor_copy(out=ln_g_cols[:], in_=ln_g_raw[:])
+            nc.vector.tensor_copy(out=ln_b_cols[:], in_=ln_b_raw[:])
+            vec_rows_f = setup.tile([P, P], F32, name="vec_rows_f")
+            nc.vector.tensor_copy(out=vec_rows_f[:], in_=vec_rows[:])
             nc.vector.quantize_mx(
                 out=w_codes[:].bitcast(FP8X4),
                 scales=w_scales[:],
                 in_=w_grouped[:].rearrange("p c t -> p (c t)"),
+            )
+            vec_ps = psum.tile([P, P], F32, name="vec_ps", tag="bank", bufs=SHARED_BANKS)
+            nc.tensor.transpose(vec_ps[:], vec_rows_f[:], ident[:])
+            nc.vector.tensor_copy(out=vec_cols[:], in_=vec_ps[:, 0:HALVES])
+            block_rows = setup.tile([P, P // CAP_DIM, CAP_DIM], F32, name="block_rows")
+            nc.vector.tensor_copy(
+                out=block_rows[:],
+                in_=ident[:, 0 : P // CAP_DIM].unsqueeze(2).to_broadcast([P, P // CAP_DIM, CAP_DIM]),
+            )
+            blocks_ps = psum.tile([P, P], F32, name="blocks_ps", tag="bank", bufs=SHARED_BANKS)
+            block_rows_2d = block_rows[:].rearrange("p n q -> p (n q)")
+            nc.tensor.matmul(out=blocks_ps[:], lhsT=block_rows_2d, rhs=block_rows_2d, start=True, stop=True)
+            nc.vector.scalar_tensor_tensor(
+                out=centre[:], in0=blocks_ps[:], scalar=-1.0 / CAP_DIM, in1=ident[:], op0=ALU.mult, op1=ALU.add
             )
 
         xt_tiles = {}
@@ -204,11 +211,13 @@ def tile_hotpatchcapsmodel_pa_t_kernel(
         def quantise_h1(i):
             codes = work.tile([P, TILES * PASSES_1 * P], U32, name="h1_codes", align_bytes=64)
             scales = work.tile([P, TILES * PASSES_1 * P], U8, name="h1_scales", align_bytes=64)
-            nc.vector.quantize_mx(
-                out=codes[:].bitcast(FP8X4),
-                scales=scales[:],
-                in_=h1_grouped[i][:].rearrange("p j g b t -> p (j g b t)"),
-            )
+            for part in parts(i):
+                cols = columns(part, PASSES_1 * P)
+                nc.vector.quantize_mx(
+                    out=codes[:, cols].bitcast(FP8X4),
+                    scales=scales[:, cols],
+                    in_=h1_grouped[i][:, part].rearrange("p j g b t -> p (j g b t)"),
+                )
             h1_q[i] = (codes, scales)
 
         def product_1(i):
@@ -237,9 +246,10 @@ def tile_hotpatchcapsmodel_pa_t_kernel(
 
         def relu(i):
             z = z_tiles[i]
-            nc.gpsimd.tensor_scalar(
-                out=z[:], in0=z[:], scalar1=F32_MAX, scalar2=0.0, op0=ALU.min, op1=ALU.max
-            )
+            for part in parts(i):
+                nc.gpsimd.tensor_scalar(
+                    out=z[:, part], in0=z[:, part], scalar1=F32_MAX, scalar2=0.0, op0=ALU.min, op1=ALU.max
+                )
 
         def row_stats(i):
             halves = small.tile([P, TILES, 6], F32, name="stat_halves")
@@ -252,9 +262,13 @@ def tile_hotpatchcapsmodel_pa_t_kernel(
 
         def rstd_1(i):
             rstd = small.tile([P, TILES], F32, name="rstd")
-            nc.scalar.activation(
-                out=rstd[:], in_=stats_tiles[i][:, :, 1], func=ACT.Abs_reciprocal_sqrt, bias=eps_col[:]
-            )
+            for part in parts(i):
+                nc.scalar.activation(
+                    out=rstd[:, part],
+                    in_=stats_tiles[i][:, part, 1],
+                    func=ACT.Abs_reciprocal_sqrt,
+                    bias=eps_col[:],
+                )
             rstds[i] = rstd
 
         def normalise(i):
@@ -277,9 +291,9 @@ def tile_hotpatchcapsmodel_pa_t_kernel(
             uT_tiles[i] = []
             for half in range(2):
                 uT = psum.tile([P, 2, TILES, P], F32, name="uT", tag="bank", bufs=SHARED_BANKS)
-                for cc in range(2):
-                    c = 2 * half + cc
-                    for j in range(TILES):
+                for j in range(TILES):
+                    for cc in range(2):
+                        c = 2 * half + cc
                         nc.tensor.transpose(uT[:, cc, j, :], u[:, j, c * P : (c + 1) * P], ident[:])
                 uT_tiles[i].append(uT)
 
@@ -287,53 +301,64 @@ def tile_hotpatchcapsmodel_pa_t_kernel(
             if half == 0:
                 planes = work.tile([P, E_CHUNKS, PAIR_ROWS], BF16, name="h_planes")
                 h_planes[i] = planes
-            for cc in range(2):
-                c = 2 * half + cc
-                nc.scalar.activation(
-                    out=h_planes[i][:, c, :],
-                    in_=uT_tiles[i][half][:, cc].rearrange("p j b -> p (j b)"),
-                    func=ACT.Identity,
-                    scale=g1_col(c),
-                    bias=beta1_col(c),
-                )
+            for part in parts(i):
+                for cc in range(2):
+                    c = 2 * half + cc
+                    nc.scalar.activation(
+                        out=h_planes[i][:, c, columns(part, P)],
+                        in_=uT_tiles[i][half][:, cc, part].rearrange("p j b -> p (j b)"),
+                        func=ACT.Identity,
+                        scale=g1_col(c),
+                        bias=beta1_col(c),
+                    )
 
         def regroup_h(i):
             grouped = work.tile([P, PAIR_ROWS, E_CHUNKS], BF16, name="h_grouped", align_bytes=64)
-            nc.scalar.copy(
-                out=grouped[:].rearrange("p (c i) t -> p c t i", i=4),
-                in_=h_planes[i][:].rearrange("p t (c i) -> p c t i", i=4),
-            )
+            for part in parts(i):
+                cols = columns(part, P)
+                nc.scalar.copy(
+                    out=grouped[:, cols].rearrange("p (c i) t -> p c t i", i=4),
+                    in_=h_planes[i][:, :, cols].rearrange("p t (c i) -> p c t i", i=4),
+                )
             h_groupeds[i] = grouped
 
         def quantise_h(i):
             codes = work.tile([P, PAIR_ROWS], U32, name="h_codes", align_bytes=64)
             scales = work.tile([P, PAIR_ROWS], U8, name="h_scales", align_bytes=64)
-            nc.vector.quantize_mx(
-                out=codes[:].bitcast(FP8X4),
-                scales=scales[:],
-                in_=h_groupeds[i][:].rearrange("p b t -> p (b t)"),
-            )
+            for part in parts(i):
+                cols = columns(part, P)
+                nc.vector.quantize_mx(
+                    out=codes[:, cols].bitcast(FP8X4),
+                    scales=scales[:, cols],
+                    in_=h_groupeds[i][:, cols].rearrange("p b t -> p (b t)"),
+                )
             h_q[i] = (codes, scales)
 
         def product_2(i):
             codes, scales = h_q[i]
             prim_ps = psum.tile([P, HALVES, PAIR_ROWS], F32, name="prim_ps", tag="prim_ps", bufs=1)
-            for h in range(HALVES):
-                nc.tensor.matmul_mx(
-                    out=prim_ps[:, h, :],
-                    lhsT=w_codes[:, h * P : (h + 1) * P].bitcast(FP8X4),
-                    lhsT_scale=w_scales[:, h * P : (h + 1) * P],
-                    rhs=codes[:].bitcast(FP8X4),
-                    rhs_scale=scales[:],
-                    start=True,
-                    stop=True,
-                )
+            for part in parts(i):
+                cols = columns(part, P)
+                for h in range(HALVES):
+                    nc.tensor.matmul_mx(
+                        out=prim_ps[:, h, cols],
+                        lhsT=w_codes[:, h * P : (h + 1) * P].bitcast(FP8X4),
+                        lhsT_scale=w_scales[:, h * P : (h + 1) * P],
+                        rhs=codes[:, cols].bitcast(FP8X4),
+                        rhs_scale=scales[:, cols],
+                        start=True,
+                        stop=True,
+                    )
             prim_banks[i] = prim_ps
 
         def capsule_bias(i):
             xT = work.tile([P, HALVES, PAIR_ROWS], F32, name="xT")
-            for h in range(HALVES):
-                nc.scalar.activation(out=xT[:, h, :], in_=prim_banks[i][:, h, :], func=ACT.Identity, bias=pc_b_col(h))
+            for part in parts(i):
+                cols = columns(part, P)
+                for h in range(HALVES):
+                    nc.scalar.activation(
+                        out=xT[:, h, cols], in_=prim_banks[i][:, h, cols], func=ACT.Identity, bias=pc_b_col(h)
+                    )
             xT_tiles[i] = xT
 
         def centre_capsules(i):
@@ -352,52 +377,72 @@ def tile_hotpatchcapsmodel_pa_t_kernel(
 
         def square_capsules(i):
             d_sq = work.tile([P, TILES * CAPS, CAP_DIM], F32, name="d_sq")
-            nc.scalar.activation(
-                out=d_sq[:].rearrange("p c q -> p (c q)"),
-                in_=d_banks[i][:].rearrange("p j c -> p (j c)"),
-                func=ACT.Square,
-            )
+            for part in parts(i):
+                nc.scalar.activation(
+                    out=d_sq[:, columns(part, CAPS)].rearrange("p c q -> p (c q)"),
+                    in_=d_banks[i][:, part].rearrange("p j c -> p (j c)"),
+                    func=ACT.Square,
+                )
             d_squares[i] = d_sq
 
         def reduce_2(i):
             d_sq_sum = small.tile([P, TILES * CAPS], F32, name="d_sq_sum")
-            nc.vector.reduce_sum(out=d_sq_sum[:], in_=d_squares[i][:], axis=AXIS_X)
+            for part in parts(i):
+                caps = columns(part, CAPS)
+                nc.vector.reduce_sum(out=d_sq_sum[:, caps], in_=d_squares[i][:, caps], axis=AXIS_X)
             d_sq_sums[i] = d_sq_sum
 
         def rstd_2(i):
             rstd2 = small.tile([P, TILES * CAPS], F32, name="rstd2")
-            nc.scalar.activation(
-                out=rstd2[:],
-                in_=d_sq_sums[i][:],
-                func=ACT.Abs_reciprocal_sqrt,
-                bias=eps_col[:],
-                scale=1.0 / CAP_DIM,
-            )
+            for part in parts(i):
+                caps = columns(part, CAPS)
+                nc.scalar.activation(
+                    out=rstd2[:, caps],
+                    in_=d_sq_sums[i][:, caps],
+                    func=ACT.Abs_reciprocal_sqrt,
+                    bias=eps_col[:],
+                    scale=1.0 / CAP_DIM,
+                )
             rstd2_tiles[i] = rstd2
 
         def scale_2(i):
             y = work.tile([P, TILES, OUT_COLS], F32, name="y")
-            nc.vector.tensor_tensor(
-                out=y[:].rearrange("p j (n q) -> p (j n) q", q=CAP_DIM),
-                in0=d_banks[i][:].rearrange("p j (n q) -> p (j n) q", q=CAP_DIM),
-                in1=rstd2_tiles[i][:].unsqueeze(2).to_broadcast([P, TILES * CAPS, CAP_DIM]),
-                op=ALU.mult,
-            )
+            for part in parts(i):
+                caps = columns(part, CAPS)
+                nc.vector.tensor_tensor(
+                    out=y[:, part].rearrange("p j (n q) -> p (j n) q", q=CAP_DIM),
+                    in0=d_banks[i][:, part].rearrange("p j (n q) -> p (j n) q", q=CAP_DIM),
+                    in1=rstd2_tiles[i][:, caps].unsqueeze(2).to_broadcast([P, caps.stop - caps.start, CAP_DIM]),
+                    op=ALU.mult,
+                )
             y_tiles[i] = y
+
+        def last_engine(i):
+            return nc.vector if i == N_PAIRS - 1 else nc.gpsimd
 
         def gain_2(i):
             y = y_tiles[i]
-            nc.gpsimd.tensor_tensor(
-                out=y[:], in0=y[:], in1=g2_all[:].unsqueeze(1).to_broadcast([P, TILES, OUT_COLS]), op=ALU.mult
-            )
+            for part in parts(i):
+                tiles = part.stop - part.start
+                last_engine(i).tensor_tensor(
+                    out=y[:, part],
+                    in0=y[:, part],
+                    in1=g2_all[:].unsqueeze(1).to_broadcast([P, tiles, OUT_COLS]),
+                    op=ALU.mult,
+                )
 
         def shift_2(i):
             y = y_tiles[i]
-            nc.gpsimd.tensor_tensor(
-                out=y[:], in0=y[:], in1=beta2_all[:].unsqueeze(1).to_broadcast([P, TILES, OUT_COLS]), op=ALU.add
-            )
-            rows = out[i * PAIR_ROWS : (i + 1) * PAIR_ROWS, :, :]
-            nc.sync.dma_start(out=rows.rearrange("(p j) n q -> p j (n q)", j=TILES), in_=y[:])
+            rows = out[i * PAIR_ROWS : (i + 1) * PAIR_ROWS, :, :].rearrange("(p j) n q -> p j (n q)", j=TILES)
+            for part in parts(i):
+                tiles = part.stop - part.start
+                last_engine(i).tensor_tensor(
+                    out=y[:, part],
+                    in0=y[:, part],
+                    in1=beta2_all[:].unsqueeze(1).to_broadcast([P, tiles, OUT_COLS]),
+                    op=ALU.add,
+                )
+                nc.sync.dma_start(out=rows[:, part], in_=y[:, part])
 
         def run(step, i, *args):
             if 0 <= i < N_PAIRS:
@@ -405,6 +450,8 @@ def tile_hotpatchcapsmodel_pa_t_kernel(
 
         for r in range(-1, N_PAIRS + 6):
             run(load, r + 2)
+            if r == W_ROUND - 1:
+                load_late_constants()
             run(normalise, r - 2)
             run(copy_h1, r)
             run(centre_capsules, r - 5)
@@ -413,7 +460,7 @@ def tile_hotpatchcapsmodel_pa_t_kernel(
             run(transpose_h1, r + 1)
             run(quantise_h1, r)
             if r == W_ROUND:
-                quantise_pc_w()
+                prepare_late_constants()
             run(square_capsules, r - 5)
             run(shift_2, r - 6)
             run(product_1, r)

@@ -109,7 +109,6 @@ def tile_hotpatchcapsmodel_pa_t_kernel(
         w_scales = const.tile([P, OUT_COLS], U8, name="w_scales", align_bytes=64)
         g2_all = const.tile([P, OUT_COLS], BF16, name="g2_all")
         beta2_all = const.tile([P, OUT_COLS], BF16, name="beta2_all")
-        w_raw = setup.tile([P, CAPS, E_CHUNKS, CAP_DIM], BF16, name="w_raw")
         ln_g_raw = setup.tile([P, E_CHUNKS], BF16, name="ln_g_raw")
         ln_b_raw = setup.tile([P, E_CHUNKS], BF16, name="ln_b_raw")
         vec_rows = setup.tile([P, P], BF16, name="vec_rows")
@@ -123,7 +122,11 @@ def tile_hotpatchcapsmodel_pa_t_kernel(
         def pc_b_col(h):
             return vec_cols[:, h : h + 1]
 
+        late = {}
+
         def load_late_constants():
+            w_raw = loads.tile([P, CAPS, E_CHUNKS, CAP_DIM], BF16, name="w_raw", tag="x_sb")
+            late["w_raw"] = w_raw
             nc.sync.dma_start(
                 out=w_raw[:].rearrange("p n t d -> p n (t d)"),
                 in_=pc_W.rearrange("n (q t) d -> q n (t d)", t=E_CHUNKS),
@@ -141,7 +144,7 @@ def tile_hotpatchcapsmodel_pa_t_kernel(
             w_grouped = setup.tile([P, OUT_COLS, E_CHUNKS], BF16, name="w_grouped", align_bytes=64)
             nc.vector.tensor_copy(
                 out=w_grouped[:].rearrange("p (n d) t -> p n d t", d=CAP_DIM),
-                in_=w_raw[:].rearrange("p n t d -> p n d t"),
+                in_=late["w_raw"][:].rearrange("p n t d -> p n d t"),
             )
             nc.vector.tensor_copy(out=ln_g_cols[:], in_=ln_g_raw[:])
             nc.vector.tensor_copy(out=ln_b_cols[:], in_=ln_b_raw[:])

from contextlib import ExitStack

import concourse.mybir as mybir
from concourse.masks import make_identity

F32 = mybir.dt.float32
BF16 = mybir.dt.bfloat16
I32 = mybir.dt.int32
U32 = mybir.dt.uint32
U8 = mybir.dt.uint8
FP8X4 = mybir.dt.float8_e4m3fn_x4
ACT = mybir.ActivationFunctionType
ALU = mybir.AluOpType
AXIS_X = mybir.AxisListType.X

P = 128
B, H1, E = 8192, 1024, 512
CAPS, CAP_DIM = 32, 8
OUT_COLS = CAPS * CAP_DIM
EPS = 1e-5
F32_MAX = 3.4028234663852886e38
K_PASS = 4 * P
PASSES_1 = H1 // K_PASS
E_CHUNKS = E // P
HALVES = OUT_COLS // P
TILES = 2
PAIR_ROWS = TILES * P
N_PAIRS = B // PAIR_ROWS
SHARED_BANKS = 5
W_ROUND = 2

FLOPS = 2 * B * (H1 * E + E * OUT_COLS)


def tile_hotpatchcapsmodel_pa_t_kernel(
    tc, h1, W2_words, W2_scales, b2, ln_g, ln_b, pc_W, pc_b, pc_g, pc_beta, out
):
    nc = tc.nc
    with ExitStack() as stack:
        const = stack.enter_context(tc.tile_pool(name="const", bufs=1))
        setup = stack.enter_context(tc.tile_pool(name="setup", bufs=1))
        loads = stack.enter_context(tc.tile_pool(name="loads", bufs=3))
        work = stack.enter_context(tc.tile_pool(name="work", bufs=3))
        small = stack.enter_context(tc.tile_pool(name="small", bufs=4))
        psum = stack.enter_context(tc.psum_pool(name="psum", bufs=1))

        def parts(i):
            if i in (0, N_PAIRS - 1):
                return [slice(j, j + 1) for j in range(TILES)]
            return [slice(0, TILES)]

        def columns(part, width):
            return slice(part.start * width, part.stop * width)

        x_tiles = {}

        def load(i):
            x_sb = loads.tile([P, TILES, H1], BF16, name="x_sb")
            rows = h1[i * PAIR_ROWS : (i + 1) * PAIR_ROWS, :].rearrange("(p j) k -> p j k", j=TILES)
            for part in parts(i):
                nc.sync.dma_start(out=x_sb[:, part], in_=rows[:, part])
            x_tiles[i] = x_sb

        eps_col = const.tile([P, 1], F32, name="eps_col")
        nc.vector.memset(eps_col[:], EPS)
        first_act = const.tile([P, 1], F32, name="first_act")
        nc.scalar.activation(out=first_act[:], in_=eps_col[:], func=ACT.Abs_reciprocal_sqrt)
        ident = const.tile([P, P], F32, name="ident")
        make_identity(nc, ident[:])

        load(0)

        w2_scales_raw = setup.tile([P, PASSES_1, E], U8, name="w2_scales_raw", align_bytes=64)
        nc.vector.memset(w2_scales_raw[:].bitcast(I32), 0)
        for quad in range(4):
            nc.sync.dma_start(
                out=w2_scales_raw[32 * quad : 32 * quad + 4, :, :].bitcast(I32),
                in_=W2_scales[:, 4 * quad : 4 * quad + 4, :].rearrange("g q n -> q g n").bitcast(I32),
            )
        w2_codes_raw = setup.tile([P, PASSES_1, E], I32, name="w2_codes_raw", align_bytes=64)
        for g in range(PASSES_1):
            nc.sync.dma_start(
                out=w2_codes_raw[:, g, :],
                in_=W2_words[g].rearrange("p n t -> p (n t)").bitcast(I32),
            )
        b2_raw = setup.tile([P, E], BF16, name="b2_raw")
        nc.sync.dma_start(out=b2_raw[:], in_=b2.partition_broadcast(P))
        w2_scales = const.tile([P, PASSES_1, E], U8, name="w2_scales", align_bytes=64)
        w2_codes = const.tile([P, PASSES_1, E], U32, name="w2_codes", align_bytes=64)
        for g in range(PASSES_1):
            nc.vector.tensor_copy(
                out=w2_scales[:, g, :].rearrange("p (t q) -> p q t", t=4),
                in_=w2_scales_raw[:, g, :].rearrange("p (q t) -> p q t", t=4),
            )
            nc.vector.tensor_copy(
                out=w2_codes[:, g, :].bitcast(I32).rearrange("p (t q) -> p t q", t=4),
                in_=w2_codes_raw[:, g, :].rearrange("p (q t) -> p t q", t=4),
            )
        b2_all = const.tile([P, E], BF16, name="b2_all")
        nc.vector.tensor_copy(
            out=b2_all[:].rearrange("p (t q) -> p t q", t=4), in_=b2_raw[:].rearrange("p (q t) -> p t q", t=4)
        )

        ln_g_cols = const.tile([P, E_CHUNKS], F32, name="ln_g_cols")
        ln_b_cols = const.tile([P, E_CHUNKS], F32, name="ln_b_cols")
        vec_cols = const.tile([P, HALVES], F32, name="vec_cols")
        centre = const.tile([P, P], F32, name="centre")
        w_codes = const.tile([P, OUT_COLS], U32, name="w_codes", align_bytes=64)
        w_scales = const.tile([P, OUT_COLS], U8, name="w_scales", align_bytes=64)
        g2_all = const.tile([P, OUT_COLS], BF16, name="g2_all")
        beta2_all = const.tile([P, OUT_COLS], BF16, name="beta2_all")
        ln_g_raw = setup.tile([P, E_CHUNKS], BF16, name="ln_g_raw")
        ln_b_raw = setup.tile([P, E_CHUNKS], BF16, name="ln_b_raw")
        vec_rows = setup.tile([P, P], BF16, name="vec_rows")

        def g1_col(c):
            return ln_g_cols[:, c : c + 1]

        def beta1_col(c):
            return ln_b_cols[:, c : c + 1]

        def pc_b_col(h):
            return vec_cols[:, h : h + 1]

        late = {}

        def load_late_constants():
            w_raw = loads.tile([P, CAPS, E_CHUNKS, CAP_DIM], BF16, name="w_raw", tag="x_sb")
            late["w_raw"] = w_raw
            nc.sync.dma_start(
                out=w_raw[:].rearrange("p n t d -> p n (t d)"),
                in_=pc_W.rearrange("n (q t) d -> q n (t d)", t=E_CHUNKS),
            )
            nc.sync.dma_start(out=ln_g_raw[:], in_=ln_g.rearrange("(q t) -> q t", t=E_CHUNKS))
            nc.sync.dma_start(out=ln_b_raw[:], in_=ln_b.rearrange("(q t) -> q t", t=E_CHUNKS))
            nc.vector.memset(vec_rows[:], 0.0)
            nc.sync.dma_start(
                out=vec_rows[0:HALVES, :], in_=pc_b.rearrange("n q -> (n q)").rearrange("(h q) -> h q", q=P)
            )
            nc.sync.dma_start(out=g2_all[:], in_=pc_g.rearrange("n q -> (n q)").partition_broadcast(P))
            nc.sync.dma_start(out=beta2_all[:], in_=pc_beta.rearrange("n q -> (n q)").partition_broadcast(P))

        def prepare_late_constants():
            w_grouped = setup.tile([P, OUT_COLS, E_CHUNKS], BF16, name="w_grouped", align_bytes=64)
            nc.vector.tensor_copy(
                out=w_grouped[:].rearrange("p (n d) t -> p n d t", d=CAP_DIM),
                in_=late["w_raw"][:].rearrange("p n t d -> p n d t"),
            )
            nc.vector.tensor_copy(out=ln_g_cols[:], in_=ln_g_raw[:])
            nc.vector.tensor_copy(out=ln_b_cols[:], in_=ln_b_raw[:])
            vec_rows_f = setup.tile([P, P], F32, name="vec_rows_f")
            nc.vector.tensor_copy(out=vec_rows_f[:], in_=vec_rows[:])
            nc.vector.quantize_mx(
                out=w_codes[:].bitcast(FP8X4),
                scales=w_scales[:],
                in_=w_grouped[:].rearrange("p c t -> p (c t)"),
            )
            vec_ps = psum.tile([P, P], F32, name="vec_ps", tag="bank", bufs=SHARED_BANKS)
            nc.tensor.transpose(vec_ps[:], vec_rows_f[:], ident[:])
            nc.vector.tensor_copy(out=vec_cols[:], in_=vec_ps[:, 0:HALVES])
            block_rows = setup.tile([P, P // CAP_DIM, CAP_DIM], F32, name="block_rows")
            nc.vector.tensor_copy(
                out=block_rows[:],
                in_=ident[:, 0 : P // CAP_DIM].unsqueeze(2).to_broadcast([P, P // CAP_DIM, CAP_DIM]),
            )
            blocks_ps = psum.tile([P, P], F32, name="blocks_ps", tag="bank", bufs=SHARED_BANKS)
            block_rows_2d = block_rows[:].rearrange("p n q -> p (n q)")
            nc.tensor.matmul(out=blocks_ps[:], lhsT=block_rows_2d, rhs=block_rows_2d, start=True, stop=True)
            nc.vector.scalar_tensor_tensor(
                out=centre[:], in0=blocks_ps[:], scalar=-1.0 / CAP_DIM, in1=ident[:], op0=ALU.mult, op1=ALU.add
            )

        xt_tiles = {}
        h1_grouped = {}
        h1_q = {}
        z_banks = {}
        z_tiles = {}
        stats_tiles = {}
        rstds = {}
        h_groupeds = {}
        d_sq_sums = {}
        y_tiles = {}
        u_tiles = {}
        uT_tiles = {}
        h_planes = {}
        h_q = {}
        prim_banks = {}
        xT_tiles = {}
        d_banks = {}
        d_squares = {}
        rstd2_tiles = {}

        def transpose_h1(i):
            x_sb = x_tiles[i]
            xt_tiles[i] = []
            for j in range(TILES):
                words = x_sb[:, j, :].bitcast(F32)
                xt = psum.tile([P, PASSES_1, 2, P], F32, name="xt", tag="bank", bufs=SHARED_BANKS)
                for g in range(PASSES_1):
                    for u in range(2):
                        nc.tensor.transpose(
                            xt[:, g, u, :], words[:, 256 * g + u : 256 * (g + 1) : 2], ident[:]
                        )
                xt_tiles[i].append(xt)

        def copy_h1(i):
            grouped = work.tile([P, TILES, PASSES_1, P, 4], BF16, name="h1_grouped", align_bytes=64)
            for j in range(TILES):
                nc.scalar.copy(
                    out=grouped[:, j].bitcast(F32), in_=xt_tiles[i][j][:].rearrange("p g u b -> p g b u")
                )
            h1_grouped[i] = grouped

        def quantise_h1(i):
            codes = work.tile([P, TILES * PASSES_1 * P], U32, name="h1_codes", align_bytes=64)
            scales = work.tile([P, TILES * PASSES_1 * P], U8, name="h1_scales", align_bytes=64)
            for part in parts(i):
                cols = columns(part, PASSES_1 * P)
                nc.vector.quantize_mx(
                    out=codes[:, cols].bitcast(FP8X4),
                    scales=scales[:, cols],
                    in_=h1_grouped[i][:, part].rearrange("p j g b t -> p (j g b t)"),
                )
            h1_q[i] = (codes, scales)

        def product_1(i):
            codes, scales = h1_q[i]
            z_banks[i] = []
            for j in range(TILES):
                z_ps = psum.tile([P, E], F32, name="z_ps", tag="bank", bufs=SHARED_BANKS)
                for g in range(PASSES_1):
                    cols = slice((j * PASSES_1 + g) * P, (j * PASSES_1 + g + 1) * P)
                    nc.tensor.matmul_mx(
                        out=z_ps[:],
                        lhsT=codes[:, cols].bitcast(FP8X4),
                        lhsT_scale=scales[:, cols],
                        rhs=w2_codes[:, g, :].bitcast(FP8X4),
                        rhs_scale=w2_scales[:, g, :],
                        start=(g == 0),
                        stop=(g == PASSES_1 - 1),
                    )
                z_banks[i].append(z_ps)

        def add_bias(i):
            z = work.tile([P, TILES, E], F32, name="z")
            for j in range(TILES):
                nc.vector.tensor_tensor(out=z[:, j, :], in0=z_banks[i][j][:], in1=b2_all[:], op=ALU.add)
            z_tiles[i] = z

        def relu(i):
            z = z_tiles[i]
            for part in parts(i):
                nc.gpsimd.tensor_scalar(
                    out=z[:, part], in0=z[:, part], scalar1=F32_MAX, scalar2=0.0, op0=ALU.min, op1=ALU.max
                )

        def row_stats(i):
            halves = small.tile([P, TILES, 6], F32, name="stat_halves")
            stats = small.tile([P, TILES, 2], F32, name="stats")
            for j in range(TILES):
                nc.vector.bn_stats(out=halves[:, j, :], in_=z_tiles[i][:, j, :])
            for j in range(TILES):
                nc.vector.bn_aggr(out=stats[:, j, :], in_=halves[:, j, :])
            stats_tiles[i] = stats

        def rstd_1(i):
            rstd = small.tile([P, TILES], F32, name="rstd")
            for part in parts(i):
                nc.scalar.activation(
                    out=rstd[:, part],
                    in_=stats_tiles[i][:, part, 1],
                    func=ACT.Abs_reciprocal_sqrt,
                    bias=eps_col[:],
                )
            rstds[i] = rstd

        def normalise(i):
            z = z_tiles[i]
            stats, rstd = stats_tiles[i], rstds[i]
            u = work.tile([P, TILES, E], F32, name="u")
            for j in range(TILES):
                nc.vector.tensor_scalar(
                    out=u[:, j, :],
                    in0=z[:, j, :],
                    scalar1=stats[:, j, 0:1],
                    scalar2=rstd[:, j : j + 1],
                    op0=ALU.subtract,
                    op1=ALU.mult,
                )
            u_tiles[i] = u

        def transpose_u(i):
            u = u_tiles[i]
            uT_tiles[i] = []
            for half in range(2):
                uT = psum.tile([P, 2, TILES, P], F32, name="uT", tag="bank", bufs=SHARED_BANKS)
                for j in range(TILES):
                    for cc in range(2):
                        c = 2 * half + cc
                        nc.tensor.transpose(uT[:, cc, j, :], u[:, j, c * P : (c + 1) * P], ident[:])
                uT_tiles[i].append(uT)

        def gain_shift(i, half):
            if half == 0:
                planes = work.tile([P, E_CHUNKS, PAIR_ROWS], BF16, name="h_planes")
                h_planes[i] = planes
            for part in parts(i):
                for cc in range(2):
                    c = 2 * half + cc
                    nc.scalar.activation(
                        out=h_planes[i][:, c, columns(part, P)],
                        in_=uT_tiles[i][half][:, cc, part].rearrange("p j b -> p (j b)"),
                        func=ACT.Identity,
                        scale=g1_col(c),
                        bias=beta1_col(c),
                    )

        def regroup_h(i):
            grouped = work.tile([P, PAIR_ROWS, E_CHUNKS], BF16, name="h_grouped", align_bytes=64)
            for part in parts(i):
                cols = columns(part, P)
                nc.scalar.copy(
                    out=grouped[:, cols].rearrange("p (c i) t -> p c t i", i=4),
                    in_=h_planes[i][:, :, cols].rearrange("p t (c i) -> p c t i", i=4),
                )
            h_groupeds[i] = grouped

        def quantise_h(i):
            codes = work.tile([P, PAIR_ROWS], U32, name="h_codes", align_bytes=64)
            scales = work.tile([P, PAIR_ROWS], U8, name="h_scales", align_bytes=64)
            for part in parts(i):
                cols = columns(part, P)
                nc.vector.quantize_mx(
                    out=codes[:, cols].bitcast(FP8X4),
                    scales=scales[:, cols],
                    in_=h_groupeds[i][:, cols].rearrange("p b t -> p (b t)"),
                )
            h_q[i] = (codes, scales)

        def product_2(i):
            codes, scales = h_q[i]
            prim_ps = psum.tile([P, HALVES, PAIR_ROWS], F32, name="prim_ps", tag="prim_ps", bufs=1)
            for part in parts(i):
                cols = columns(part, P)
                for h in range(HALVES):
                    nc.tensor.matmul_mx(
                        out=prim_ps[:, h, cols],
                        lhsT=w_codes[:, h * P : (h + 1) * P].bitcast(FP8X4),
                        lhsT_scale=w_scales[:, h * P : (h + 1) * P],
                        rhs=codes[:, cols].bitcast(FP8X4),
                        rhs_scale=scales[:, cols],
                        start=True,
                        stop=True,
                    )
            prim_banks[i] = prim_ps

        def capsule_bias(i):
            xT = work.tile([P, HALVES, PAIR_ROWS], F32, name="xT")
            for part in parts(i):
                cols = columns(part, P)
                for h in range(HALVES):
                    nc.scalar.activation(
                        out=xT[:, h, cols], in_=prim_banks[i][:, h, cols], func=ACT.Identity, bias=pc_b_col(h)
                    )
            xT_tiles[i] = xT

        def centre_capsules(i):
            xT = xT_tiles[i]
            d_ps = psum.tile([P, TILES, OUT_COLS], F32, name="d_ps", tag="d_ps", bufs=2)
            for j in range(TILES):
                for h in range(HALVES):
                    nc.tensor.matmul(
                        out=d_ps[:, j, h * P : (h + 1) * P],
                        lhsT=xT[:, h, j * P : (j + 1) * P],
                        rhs=centre[:],
                        start=True,
                        stop=True,
                    )
            d_banks[i] = d_ps

        def square_capsules(i):
            d_sq = work.tile([P, TILES * CAPS, CAP_DIM], F32, name="d_sq")
            for part in parts(i):
                nc.scalar.activation(
                    out=d_sq[:, columns(part, CAPS)].rearrange("p c q -> p (c q)"),
                    in_=d_banks[i][:, part].rearrange("p j c -> p (j c)"),
                    func=ACT.Square,
                )
            d_squares[i] = d_sq

        def reduce_2(i):
            d_sq_sum = small.tile([P, TILES * CAPS], F32, name="d_sq_sum")
            for part in parts(i):
                caps = columns(part, CAPS)
                nc.vector.reduce_sum(out=d_sq_sum[:, caps], in_=d_squares[i][:, caps], axis=AXIS_X)
            d_sq_sums[i] = d_sq_sum

        def rstd_2(i):
            rstd2 = small.tile([P, TILES * CAPS], F32, name="rstd2")
            for part in parts(i):
                caps = columns(part, CAPS)
                nc.scalar.activation(
                    out=rstd2[:, caps],
                    in_=d_sq_sums[i][:, caps],
                    func=ACT.Abs_reciprocal_sqrt,
                    bias=eps_col[:],
                    scale=1.0 / CAP_DIM,
                )
            rstd2_tiles[i] = rstd2

        def scale_2(i):
            y = work.tile([P, TILES, OUT_COLS], F32, name="y")
            for part in parts(i):
                caps = columns(part, CAPS)
                nc.vector.tensor_tensor(
                    out=y[:, part].rearrange("p j (n q) -> p (j n) q", q=CAP_DIM),
                    in0=d_banks[i][:, part].rearrange("p j (n q) -> p (j n) q", q=CAP_DIM),
                    in1=rstd2_tiles[i][:, caps].unsqueeze(2).to_broadcast([P, caps.stop - caps.start, CAP_DIM]),
                    op=ALU.mult,
                )
            y_tiles[i] = y

        def last_engine(i):
            return nc.vector if i == N_PAIRS - 1 else nc.gpsimd

        def gain_2(i):
            y = y_tiles[i]
            for part in parts(i):
                tiles = part.stop - part.start
                last_engine(i).tensor_tensor(
                    out=y[:, part],
                    in0=y[:, part],
                    in1=g2_all[:].unsqueeze(1).to_broadcast([P, tiles, OUT_COLS]),
                    op=ALU.mult,
                )

        def shift_2(i):
            y = y_tiles[i]
            rows = out[i * PAIR_ROWS : (i + 1) * PAIR_ROWS, :, :].rearrange("(p j) n q -> p j (n q)", j=TILES)
            for part in parts(i):
                tiles = part.stop - part.start
                last_engine(i).tensor_tensor(
                    out=y[:, part],
                    in0=y[:, part],
                    in1=beta2_all[:].unsqueeze(1).to_broadcast([P, tiles, OUT_COLS]),
                    op=ALU.add,
                )
                nc.sync.dma_start(out=rows[:, part], in_=y[:, part])

        def run(step, i, *args):
            if 0 <= i < N_PAIRS:
                step(i, *args)

        for r in range(-1, N_PAIRS + 6):
            run(load, r + 2)
            if r == W_ROUND - 1:
                load_late_constants()
            run(normalise, r - 2)
            run(copy_h1, r)
            run(centre_capsules, r - 5)
            run(gain_2, r - 6)
            run(relu, r - 1)
            run(transpose_h1, r + 1)
            run(quantise_h1, r)
            if r == W_ROUND:
                prepare_late_constants()
            run(square_capsules, r - 5)
            run(shift_2, r - 6)
            run(product_1, r)
            run(regroup_h, r - 4)
            run(gain_shift, r - 3, 0)
            run(gain_shift, r - 3, 1)
            run(reduce_2, r - 5)
            run(quantise_h, r - 4)
            run(product_2, r - 4)
            run(rstd_2, r - 5)
            run(transpose_u, r - 2)
            run(row_stats, r - 1)
            run(scale_2, r - 5)
            run(add_bias, r)
            run(capsule_bias, r - 4)
            run(rstd_1, r - 1)
